import numpy as np
import ml_dtypes


def mxq(x, axis, fmt="e4m3"):
    dtype, down = {"e4m3": (ml_dtypes.float8_e4m3fn, 7), "e5m2": (ml_dtypes.float8_e5m2, 14)}[fmt]
    v = np.moveaxis(np.asarray(x, np.float32).astype(ml_dtypes.bfloat16).astype(np.float64), axis, -1)
    blocks = v.reshape(v.shape[:-1] + (-1, 32))
    amax = np.abs(blocks).max(-1, keepdims=True)
    byte = np.maximum(np.where(amax > 0, np.frexp(amax)[1] - 1 + 127, 0) - down, 1)
    scale = np.exp2(byte - 127.0)
    codes = (blocks / scale).astype(np.float32).astype(dtype).astype(np.float64)
    return np.moveaxis((codes * scale).reshape(v.shape), -1, axis)


WIDE = False


def mx_kscale(k):
    if not WIDE:
        return np.ones(k)
    levels = np.array([10, -10, 5, -5, 0])
    a = np.random.permutation(np.resize(levels, k // 512 * 4)).reshape(k // 512, 4)
    idx = np.arange(k)
    return np.exp2(a[idx // 512, idx % 128 // 32])


BF16 = ml_dtypes.bfloat16


def bf(x):
    return np.asarray(x, np.float32).astype(BF16)


def f64(x):
    return np.asarray(x).astype(np.float64)


E2M1 = np.array([0.0, 0.5, 1.0, 1.5, 2.0, 3.0, 4.0, 6.0, -0.0, -0.5, -1.0, -1.5, -2.0, -3.0, -4.0, -6.0])


def pack_weight(w, fmt):
    k, n = w.shape
    w = f64(bf(w)).reshape(k // 32, 32, n)
    amax = np.abs(w).max(1)
    if fmt == "e4m3":
        byte = np.frexp(amax)[1] - 1 + 127 - 7
    else:
        mant, ex = np.frexp(amax / 6.0)
        byte = np.where(mant > 0.5, ex, ex - 1) + 127
    byte = np.clip(np.where(amax > 0, byte, 1), 1, 254)
    scaled = (w * np.exp2(127.0 - byte)[:, None, :]).reshape(k, n).astype(np.float32)
    by_word = np.ascontiguousarray(scaled.reshape(k // 512, 128, 4, n).transpose(0, 1, 3, 2))
    if fmt == "e4m3":
        words = by_word.astype(ml_dtypes.float8_e4m3fn).view(np.uint8)
    else:
        c = by_word.astype(ml_dtypes.float4_e2m1fn).view(np.uint8) & 0xF
        words = c[..., 0::2] | (c[..., 1::2] << 4)
    return np.ascontiguousarray(words), np.ascontiguousarray(byte.astype(np.uint8).reshape(k // 512, 16, n))


def unpack_weight(words, scales, fmt):
    g, p, n, _ = words.shape
    if fmt == "e4m3":
        vals = np.ascontiguousarray(words).view(ml_dtypes.float8_e4m3fn).astype(np.float64)
    else:
        nib = np.empty((g, p, n, 4), np.uint8)
        nib[..., 0::2] = words & 0xF
        nib[..., 1::2] = words >> 4
        vals = E2M1[nib]
    vals = vals * np.repeat(np.exp2(scales.astype(np.float64) - 127.0), 8, axis=1)[..., None]
    return vals.transpose(0, 1, 3, 2).reshape(g * 512, n)


B, S, DIM, N_HEADS, HEAD_DIM, F = 2, 64, 8192, 8, 128, 4096
QD = N_HEADS * HEAD_DIM
THETA = 10000.0
EPS = 1e-6
FMT = "e4m3"


def rms_norm(x, w):
    return x * (1.0 / np.sqrt(np.mean(x * x, axis=-1, keepdims=True) + EPS)) * w


def rope_tables():
    inv = 1.0 / THETA ** (np.arange(0, HEAD_DIM, 2) / HEAD_DIM)
    freqs = np.outer(np.arange(S), inv)
    return np.cos(freqs), np.sin(freqs)


def rot(u, cos, sin):
    c = cos[None, :, None, :]
    s = sin[None, :, None, :]
    ur, ui = u[..., 0::2], u[..., 1::2]
    yr = ur * c - ui * s
    yi = ur * s + ui * c
    return np.stack([yr, yi], axis=-1).reshape(u.shape)


def setup_inputs():
    s = mx_kscale(DIM)
    sc = 1.0 / np.sqrt(DIM)
    quiet = np.where(np.random.random((B, S, 1)) < 0.125, 1e-3, 1.0)
    x = bf(np.random.standard_normal((B, S, DIM)) * quiet)
    attn_norm_w = bf((1.0 + 0.1 * np.random.standard_normal(DIM)) * s)
    wq_words, wq_scales = pack_weight(np.random.standard_normal((DIM, QD)) * sc / s[:, None], FMT)
    wk_words, wk_scales = pack_weight(np.random.standard_normal((DIM, QD)) * sc / s[:, None], FMT)
    wv_words, wv_scales = pack_weight(np.random.standard_normal((DIM, QD)) * sc / s[:, None], FMT)
    return {"x": x,
            "attn_norm_w": attn_norm_w,
            "wq_words": wq_words, "wq_scales": wq_scales,
            "wk_words": wk_words, "wk_scales": wk_scales,
            "wv_words": wv_words, "wv_scales": wv_scales}


def reference(x, attn_norm_w, wq_words, wq_scales, wk_words, wk_scales, wv_words, wv_scales):
    h = rms_norm(f64(x), f64(attn_norm_w))
    hq = mxq(h, 2, "e4m3")
    q = (hq @ unpack_weight(wq_words, wq_scales, FMT)).reshape(B, S, N_HEADS, HEAD_DIM)
    k = (hq @ unpack_weight(wk_words, wk_scales, FMT)).reshape(B, S, N_HEADS, HEAD_DIM)
    v = (hq @ unpack_weight(wv_words, wv_scales, FMT)).reshape(B, S, N_HEADS, HEAD_DIM)
    cos, sin = rope_tables()
    q = rot(q, cos, sin)
    k = rot(k, cos, sin)
    return q.transpose(0, 2, 1, 3), k.transpose(0, 2, 1, 3), v.transpose(0, 2, 1, 3)

@@ -1,0 +1,240 @@
+import math
+from contextlib import ExitStack
+
+import concourse.mybir as mybir
+from concourse.masks import make_identity
+
+F32 = mybir.dt.float32
+BF16 = mybir.dt.bfloat16
+I32 = mybir.dt.int32
+U32 = mybir.dt.uint32
+U8 = mybir.dt.uint8
+FP8X4 = mybir.dt.float8_e4m3fn_x4
+ALU = mybir.AluOpType
+ACT = mybir.ActivationFunctionType
+
+BATCH = 2
+SEQ = 64
+DIM = 8192
+HEADS = 8
+HEAD_DIM = 128
+THETA = 10000.0
+EPS = 1e-6
+
+P = 128
+PACK = 4
+K_PASS = P * PACK
+PASSES = DIM // K_PASS
+OUT_COLS = HEADS * HEAD_DIM
+BANK_COLS = 512
+BANKS = OUT_COLS // BANK_COLS
+BANK_HEADS = BANK_COLS // HEAD_DIM
+PAIRS = HEAD_DIM // 2
+DOUBLINGS = 6
+GROUP = 4
+GROUPS = PASSES // GROUP
+QUADRANT = 32
+QUADRANTS = P // QUADRANT
+QUADRANT_ROWS = 4
+X_CHUNKS = 4
+X_CHUNK = DIM // X_CHUNKS
+STREAM_BUFS = 32
+
+ROUND_MAGIC = 1.5 * 2.0**23
+
+FLOPS = 2 * P * DIM * 3 * OUT_COLS
+
+assert P == BATCH * SEQ
+assert 2**DOUBLINGS == PAIRS
+
+
+def rope_table(nc, const):
+    partition = const.tile([P, 1], I32)
+    nc.gpsimd.iota(partition[:], pattern=[[0, 1]], base=0, channel_multiplier=1)
+    position = const.tile([P, 1], I32)
+    nc.vector.tensor_single_scalar(out=position[:], in_=partition[:], scalar=1, op=ALU.arith_shift_right)
+
+    turns = const.tile([P, PAIRS], F32)
+    nc.vector.tensor_scalar(
+        out=turns[:, 0:1], in0=position[:], scalar1=1.0 / (2.0 * math.pi), scalar2=None, op0=ALU.mult
+    )
+    ratio = THETA ** (-2.0 / HEAD_DIM)
+    for step in range(DOUBLINGS):
+        width = 2**step
+        nc.vector.tensor_scalar(
+            out=turns[:, width : 2 * width], in0=turns[:, 0:width], scalar1=ratio**width, scalar2=None, op0=ALU.mult
+        )
+
+    twice = turns[:].unsqueeze(2).to_broadcast([P, PAIRS, 2])
+    phase = const.tile([P, 2, PAIRS, 2], F32)
+    nc.vector.tensor_scalar(out=phase[:, 0], in0=twice, scalar1=0.25, scalar2=None, op0=ALU.add)
+    nc.vector.tensor_copy(out=phase[:, 1], in_=twice)
+    whole = const.tile([P, 2, PAIRS, 2], F32)
+    nc.vector.tensor_scalar(
+        out=whole[:], in0=phase[:], scalar1=ROUND_MAGIC, scalar2=ROUND_MAGIC, op0=ALU.add, op1=ALU.subtract
+    )
+    fraction = const.tile([P, 2, PAIRS, 2], F32)
+    nc.vector.tensor_tensor(out=fraction[:], in0=phase[:], in1=whole[:], op=ALU.subtract)
+    table = const.tile([P, 2, PAIRS, 2], F32)
+    nc.scalar.activation(out=table[:], in_=fraction[:], func=ACT.Sin, scale=2.0 * math.pi)
+    return table
+
+
+def load_scale_planes(nc, planes, scales):
+    for a in range(GROUPS):
+        for quadrant in range(QUADRANTS):
+            first = QUADRANT * quadrant
+            rows = slice(QUADRANT_ROWS * quadrant, QUADRANT_ROWS * (quadrant + 1))
+            nc.gpsimd.dma_start(
+                out=planes[first : first + GROUP * QUADRANT_ROWS, a, :].bitcast(F32),
+                in_=scales[GROUP * a : GROUP * (a + 1), rows, :].bitcast(F32),
+            )
+
+
+def rotate_bank(nc, tail, table, acc, y):
+    def over_heads(cos_or_sin):
+        return cos_or_sin.rearrange("m j e -> m (j e)").unsqueeze(1).to_broadcast([P, BANK_HEADS, HEAD_DIM])
+
+    def pairs(tile_ap):
+        return tile_ap.rearrange("m h (j e) -> m (h j) e", e=2)
+
+    u = acc[:].rearrange("m (h f) -> m h f", f=HEAD_DIM)
+    u_cos = tail.tile([P, BANK_HEADS, HEAD_DIM], F32)
+    nc.vector.tensor_tensor(out=u_cos[:], in0=u, in1=over_heads(table[:, 0]), op=ALU.mult)
+    u_sin = tail.tile([P, BANK_HEADS, HEAD_DIM], F32)
+    nc.vector.tensor_tensor(out=u_sin[:], in0=u, in1=over_heads(table[:, 1]), op=ALU.mult)
+    nc.vector.tensor_tensor(
+        out=pairs(y[:])[:, :, 0], in0=pairs(u_cos[:])[:, :, 0], in1=pairs(u_sin[:])[:, :, 1], op=ALU.subtract
+    )
+    nc.vector.tensor_tensor(
+        out=pairs(y[:])[:, :, 1], in0=pairs(u_cos[:])[:, :, 1], in1=pairs(u_sin[:])[:, :, 0], op=ALU.add
+    )
+
+
+def tile_flexattentionblock_pa_k_kernel(
+    tc, x, attn_norm_w, wq_words, wq_scales, wk_words, wk_scales, wv_words, wv_scales, out_0, out_1, out_2
+):
+    nc = tc.nc
+    with ExitStack() as ctx:
+        ctx.enter_context(tc.manual_schedule())
+        const = ctx.enter_context(tc.tile_pool(name="const", bufs=1))
+        head = ctx.enter_context(tc.tile_pool(name="head", bufs=3))
+        stream = ctx.enter_context(tc.tile_pool(name="stream", bufs=STREAM_BUFS))
+        tail = ctx.enter_context(tc.tile_pool(name="tail", bufs=2))
+        psum_t = ctx.enter_context(tc.psum_pool(name="psum_t", bufs=2))
+        psum_acc = ctx.enter_context(tc.psum_pool(name="psum_acc", bufs=1))
+
+        gain_rows = const.tile([PASSES, K_PASS], BF16)
+        nc.sync.dma_start(out=gain_rows[:], in_=attn_norm_w.rearrange("(g c) -> g c", c=K_PASS))
+        x_sb = const.tile([P, DIM], BF16)
+        x_tokens = x.rearrange("b s d -> s b d")
+        for c in range(X_CHUNKS):
+            cols = slice(c * X_CHUNK, (c + 1) * X_CHUNK)
+            nc.sync.dma_start(out=x_sb[:, cols], in_=x_tokens[:, :, cols])
+
+        scale_inputs = {"q": wq_scales, "k": wk_scales, "v": wv_scales}
+        planes = {}
+        for name in ("q", "k", "v"):
+            planes[name] = const.tile([P, GROUPS, OUT_COLS], U8, align_bytes=64, name="planes_%s" % name)
+            nc.vector.memset(planes[name][:].bitcast(I32), 0)
+
+        table = rope_table(nc, const)
+        identity = const.tile([P, P], F32)
+        make_identity(nc, identity[:])
+        for name in ("q", "k", "v"):
+            load_scale_planes(nc, planes[name], scale_inputs[name])
+
+        gain_sorted = const.tile([P, PACK, P], F32)
+        nc.vector.memset(gain_sorted[:], 0.0)
+        nc.vector.tensor_copy(
+            out=gain_sorted[0:PASSES].rearrange("g t p -> g p t"),
+            in_=gain_rows[:].rearrange("g (p t) -> g p t", t=PACK),
+        )
+        gain_t = psum_t.tile([P, PACK, P], F32, tag="transposed")
+        for t in range(PACK):
+            nc.tensor.transpose(out=gain_t[:, t, :], in_=gain_sorted[:, t, :], identity=identity[:])
+        gain = const.tile([P, PASSES, PACK], F32)
+        nc.vector.tensor_copy(out=gain[:], in_=gain_t[:, :, 0:PASSES].rearrange("p t g -> p g t"))
+
+        square_sums = const.tile([P, X_CHUNKS], F32)
+        for c in range(X_CHUNKS):
+            squares = head.tile([P, X_CHUNK], BF16)
+            nc.scalar.activation(
+                out=squares[:],
+                in_=x_sb[:, c * X_CHUNK : (c + 1) * X_CHUNK],
+                func=ACT.Square,
+                accum_out=square_sums[:, c : c + 1],
+            )
+        square_sum = const.tile([P, 1], F32)
+        nc.vector.tensor_reduce(out=square_sum[:], in_=square_sums[:], axis=mybir.AxisListType.X, op=ALU.add)
+        mean_square = const.tile([P, 1], F32)
+        nc.vector.tensor_scalar(
+            out=mean_square[:], in0=square_sum[:], scalar1=1.0 / DIM, scalar2=EPS, op0=ALU.mult, op1=ALU.add
+        )
+        rms = const.tile([P, 1], F32)
+        nc.scalar.activation(out=rms[:], in_=mean_square[:], func=ACT.Sqrt)
+        inv_rms = const.tile([P, 1], F32)
+        nc.vector.reciprocal(out=inv_rms[:], in_=rms[:])
+
+        h_words = const.tile([P, PASSES, P], U32, align_bytes=64)
+        h_planes = const.tile([P, PASSES, P], U8, align_bytes=64)
+        for a in range(GROUPS):
+            h_bf16 = head.tile([P, GROUP, P, PACK], BF16, align_bytes=64)
+            for j in range(GROUP):
+                g = GROUP * a + j
+                x_scaled = head.tile([P, PACK, P], F32)
+                nc.scalar.activation(
+                    out=x_scaled[:].rearrange("m t p -> m p t"),
+                    in_=x_sb[:, g * K_PASS : (g + 1) * K_PASS].rearrange("m (p t) -> m p t", t=PACK),
+                    func=ACT.Copy,
+                    scale=inv_rms[:, 0:1],
+                )
+                x_t = psum_t.tile([P, PACK, P], F32, tag="transposed")
+                for t in range(PACK):
+                    nc.tensor.transpose(out=x_t[:, t, :], in_=x_scaled[:, t, :], identity=identity[:])
+                nc.vector.tensor_tensor(
+                    out=h_bf16[:, j],
+                    in0=x_t[:].rearrange("p t m -> p m t"),
+                    in1=gain[:, g, :].unsqueeze(1).to_broadcast([P, P, PACK]),
+                    op=ALU.mult,
+                )
+            group = slice(GROUP * a, GROUP * (a + 1))
+            nc.vector.quantize_mx(
+                out=h_words[:, group, :].rearrange("p g m -> p (g m)").bitcast(FP8X4),
+                scales=h_planes[:, group, :].rearrange("p g m -> p (g m)"),
+                in_=h_bf16[:].rearrange("p j m t -> p (j m t)"),
+            )
+
+        for name, words, out, store_queue in (
+            ("q", wq_words, out_0, nc.scalar),
+            ("k", wk_words, out_1, nc.scalar),
+            ("v", wv_words, out_2, nc.sync),
+        ):
+            accs = [psum_acc.tile([P, BANK_COLS], F32, name="acc_%s_%d" % (name, bank)) for bank in range(BANKS)]
+            for g in range(PASSES):
+                w_words = stream.tile([P, OUT_COLS], U32, align_bytes=64)
+                nc.sync.dma_start(
+                    out=w_words[:].bitcast(I32), in_=words[g].rearrange("p n t -> p (n t)").bitcast(I32)
+                )
+                for bank in range(BANKS):
+                    cols = slice(bank * BANK_COLS, (bank + 1) * BANK_COLS)
+                    nc.tensor.matmul_mx(
+                        out=accs[bank][:],
+                        lhsT=h_words[:, g, :].bitcast(FP8X4),
+                        lhsT_scale=h_planes[:, g, :],
+                        rhs=w_words[:, cols].bitcast(FP8X4),
+                        rhs_scale=planes[name][QUADRANT_ROWS * (g % GROUP) : P, g // GROUP, cols],
+                        start=(g == 0),
+                        stop=(g == PASSES - 1),
+                    )
+            for bank in range(BANKS):
+                y = tail.tile([P, BANK_HEADS, HEAD_DIM], F32)
+                if name != "v":
+                    rotate_bank(nc, tail, table, accs[bank], y)
+                elif bank == 0:
+                    nc.vector.tensor_copy(out=y[:].rearrange("m h f -> m (h f)"), in_=accs[bank][:])
+                else:
+                    nc.scalar.copy(out=y[:].rearrange("m h f -> m (h f)"), in_=accs[bank][:])
+                heads = slice(bank * BANK_HEADS, (bank + 1) * BANK_HEADS)
+                for b in range(BATCH):
+                    store_queue.dma_start(out=out[b, heads].rearrange("h s f -> s h f"), in_=y[b:P:BATCH])

@@ -104,10 +104,10 @@ def rotate_bank(nc, tail, table, acc, y):
     u_sin = tail.tile([P, BANK_HEADS, HEAD_DIM], F32)
     nc.vector.tensor_tensor(out=u_sin[:], in0=u, in1=over_heads(table[:, 1]), op=ALU.mult)
     nc.vector.tensor_tensor(
-        out=pairs(y[:])[:, :, 0], in0=pairs(u_cos[:])[:, :, 0], in1=pairs(u_sin[:])[:, :, 1], op=ALU.subtract
+        out=pairs(y)[:, :, 0], in0=pairs(u_cos[:])[:, :, 0], in1=pairs(u_sin[:])[:, :, 1], op=ALU.subtract
     )
     nc.vector.tensor_tensor(
-        out=pairs(y[:])[:, :, 1], in0=pairs(u_cos[:])[:, :, 1], in1=pairs(u_sin[:])[:, :, 0], op=ALU.add
+        out=pairs(y)[:, :, 1], in0=pairs(u_cos[:])[:, :, 1], in1=pairs(u_sin[:])[:, :, 0], op=ALU.add
     )
 
 
@@ -205,11 +205,8 @@ def tile_flexattentionblock_pa_k_kernel(
                 in_=h_bf16[:].rearrange("p j m t -> p (j m t)"),
             )
 
-        for name, words, out, store_queue in (
-            ("q", wq_words, out_0, nc.scalar),
-            ("k", wk_words, out_1, nc.scalar),
-            ("v", wv_words, out_2, nc.sync),
-        ):
+        results = {}
+        for name, words in (("q", wq_words), ("k", wk_words), ("v", wv_words)):
             accs = [psum_acc.tile([P, BANK_COLS], F32, name="acc_%s_%d" % (name, bank)) for bank in range(BANKS)]
             for g in range(PASSES):
                 w_words = stream.tile([P, OUT_COLS], U32, align_bytes=64)
@@ -227,14 +224,16 @@ def tile_flexattentionblock_pa_k_kernel(
                         start=(g == 0),
                         stop=(g == PASSES - 1),
                     )
+            results[name] = const.tile([P, HEADS, HEAD_DIM], F32, name="result_%s" % name)
             for bank in range(BANKS):
-                y = tail.tile([P, BANK_HEADS, HEAD_DIM], F32)
+                y = results[name][:, bank * BANK_HEADS : (bank + 1) * BANK_HEADS, :]
                 if name != "v":
                     rotate_bank(nc, tail, table, accs[bank], y)
                 elif bank == 0:
-                    nc.vector.tensor_copy(out=y[:].rearrange("m h f -> m (h f)"), in_=accs[bank][:])
+                    nc.vector.tensor_copy(out=y.rearrange("m h f -> m (h f)"), in_=accs[bank][:])
                 else:
-                    nc.scalar.copy(out=y[:].rearrange("m h f -> m (h f)"), in_=accs[bank][:])
-                heads = slice(bank * BANK_HEADS, (bank + 1) * BANK_HEADS)
-                for b in range(BATCH):
-                    store_queue.dma_start(out=out[b, heads].rearrange("h s f -> s h f"), in_=y[b:P:BATCH])
+                    nc.scalar.copy(out=y.rearrange("m h f -> m (h f)"), in_=accs[bank][:])
+
+        for name, out in (("q", out_0), ("k", out_1), ("v", out_2)):
+            for b in range(BATCH):
+                nc.sync.dma_start(out=out[b].rearrange("h s f -> s h f"), in_=results[name][b:P:BATCH])

@@ -25,17 +25,19 @@ P = 128
 PACK = 4
 K_PASS = P * PACK
 PASSES = DIM // K_PASS
+BLOCK_ROWS = 8
 OUT_COLS = HEADS * HEAD_DIM
 BANK_COLS = 512
 BANKS = OUT_COLS // BANK_COLS
 BANK_HEADS = BANK_COLS // HEAD_DIM
 PAIRS = HEAD_DIM // 2
 DOUBLINGS = 6
-GROUP = 4
-GROUPS = PASSES // GROUP
 QUADRANT = 32
 QUADRANTS = P // QUADRANT
 QUADRANT_ROWS = 4
+OFFSETS = 4
+PLANES = PASSES // OFFSETS
+QUANTISED_TOGETHER = 4
 X_CHUNKS = 4
 X_CHUNK = DIM // X_CHUNKS
 STREAM_BUFS = 32
@@ -81,14 +83,13 @@ def rope_table(nc, const):
 
 
 def load_scale_planes(nc, planes, scales):
-    for a in range(GROUPS):
-        for quadrant in range(QUADRANTS):
-            first = QUADRANT * quadrant
-            rows = slice(QUADRANT_ROWS * quadrant, QUADRANT_ROWS * (quadrant + 1))
-            nc.gpsimd.dma_start(
-                out=planes[first : first + GROUP * QUADRANT_ROWS, a, :].bitcast(F32),
-                in_=scales[GROUP * a : GROUP * (a + 1), rows, :].bitcast(F32),
-            )
+    for quadrant in range(QUADRANTS):
+        first = QUADRANT * quadrant
+        groups = slice(QUADRANT_ROWS * quadrant, QUADRANT_ROWS * (quadrant + 1))
+        nc.gpsimd.dma_start(
+            out=planes[first : first + OFFSETS * QUADRANT_ROWS].rearrange("m f n -> m (f n)").bitcast(F32),
+            in_=scales[groups].rearrange("r (j f) n -> j r (f n)", f=PLANES).bitcast(F32),
+        )
 
 
 def rotate_bank(nc, tail, table, acc, y):
@@ -125,7 +126,11 @@ def tile_flexattentionblock_pa_k_kernel(
         psum_acc = ctx.enter_context(tc.psum_pool(name="psum_acc", bufs=1))
 
         gain_rows = const.tile([PASSES, K_PASS], BF16)
-        nc.sync.dma_start(out=gain_rows[:], in_=attn_norm_w.rearrange("(g c) -> g c", c=K_PASS))
+        block = BLOCK_ROWS * PACK
+        nc.sync.dma_start(
+            out=gain_rows[:].rearrange("c (g u) -> c g u", u=block),
+            in_=attn_norm_w.rearrange("(g c u) -> c g u", c=PASSES, u=block),
+        )
         x_sb = const.tile([P, DIM], BF16)
         x_tokens = x.rearrange("b s d -> s b d")
         for c in range(X_CHUNKS):
@@ -135,7 +140,7 @@ def tile_flexattentionblock_pa_k_kernel(
         scale_inputs = {"q": wq_scales, "k": wk_scales, "v": wv_scales}
         planes = {}
         for name in ("q", "k", "v"):
-            planes[name] = const.tile([P, GROUPS, OUT_COLS], U8, align_bytes=64, name="planes_%s" % name)
+            planes[name] = const.tile([P, PLANES, OUT_COLS], U8, align_bytes=64, name="planes_%s" % name)
             nc.vector.memset(planes[name][:].bitcast(I32), 0)
 
         table = rope_table(nc, const)
@@ -147,14 +152,14 @@ def tile_flexattentionblock_pa_k_kernel(
         gain_sorted = const.tile([P, PACK, P], F32)
         nc.vector.memset(gain_sorted[:], 0.0)
         nc.vector.tensor_copy(
-            out=gain_sorted[0:PASSES].rearrange("g t p -> g p t"),
-            in_=gain_rows[:].rearrange("g (p t) -> g p t", t=PACK),
+            out=gain_sorted[0:PASSES].rearrange("c t p -> c p t"),
+            in_=gain_rows[:].rearrange("c (p t) -> c p t", t=PACK),
         )
         gain_t = psum_t.tile([P, PACK, P], F32, tag="transposed")
         for t in range(PACK):
             nc.tensor.transpose(out=gain_t[:, t, :], in_=gain_sorted[:, t, :], identity=identity[:])
         gain = const.tile([P, PASSES, PACK], F32)
-        nc.vector.tensor_copy(out=gain[:], in_=gain_t[:, :, 0:PASSES].rearrange("p t g -> p g t"))
+        nc.vector.tensor_copy(out=gain[:], in_=gain_t[:, :, 0:PASSES].rearrange("p t c -> p c t"))
 
         square_sums = const.tile([P, X_CHUNKS], F32)
         for c in range(X_CHUNKS):
@@ -178,14 +183,15 @@ def tile_flexattentionblock_pa_k_kernel(
 
         h_words = const.tile([P, PASSES, P], U32, align_bytes=64)
         h_planes = const.tile([P, PASSES, P], U8, align_bytes=64)
-        for a in range(GROUPS):
-            h_bf16 = head.tile([P, GROUP, P, PACK], BF16, align_bytes=64)
-            for j in range(GROUP):
-                g = GROUP * a + j
+        x_passes = x_sb[:].rearrange("m (g c i t) -> m c g i t", c=PASSES, i=BLOCK_ROWS, t=PACK)
+        for first_pass in range(0, PASSES, QUANTISED_TOGETHER):
+            h_bf16 = head.tile([P, QUANTISED_TOGETHER, P, PACK], BF16, align_bytes=64)
+            for j in range(QUANTISED_TOGETHER):
+                c = first_pass + j
                 x_scaled = head.tile([P, PACK, P], F32)
                 nc.scalar.activation(
-                    out=x_scaled[:].rearrange("m t p -> m p t"),
-                    in_=x_sb[:, g * K_PASS : (g + 1) * K_PASS].rearrange("m (p t) -> m p t", t=PACK),
+                    out=x_scaled[:].rearrange("m t (g i) -> m g i t", i=BLOCK_ROWS),
+                    in_=x_passes[:, c],
                     func=ACT.Copy,
                     scale=inv_rms[:, 0:1],
                 )
@@ -195,34 +201,36 @@ def tile_flexattentionblock_pa_k_kernel(
                 nc.vector.tensor_tensor(
                     out=h_bf16[:, j],
                     in0=x_t[:].rearrange("p t m -> p m t"),
-                    in1=gain[:, g, :].unsqueeze(1).to_broadcast([P, P, PACK]),
+                    in1=gain[:, c, :].unsqueeze(1).to_broadcast([P, P, PACK]),
                     op=ALU.mult,
                 )
-            group = slice(GROUP * a, GROUP * (a + 1))
+            together = slice(first_pass, first_pass + QUANTISED_TOGETHER)
             nc.vector.quantize_mx(
-                out=h_words[:, group, :].rearrange("p g m -> p (g m)").bitcast(FP8X4),
-                scales=h_planes[:, group, :].rearrange("p g m -> p (g m)"),
+                out=h_words[:, together, :].rearrange("p c m -> p (c m)").bitcast(FP8X4),
+                scales=h_planes[:, together, :].rearrange("p c m -> p (c m)"),
                 in_=h_bf16[:].rearrange("p j m t -> p (j m t)"),
             )
 
         results = {}
         for name, words in (("q", wq_words), ("k", wk_words), ("v", wv_words)):
             accs = [psum_acc.tile([P, BANK_COLS], F32, name="acc_%s_%d" % (name, bank)) for bank in range(BANKS)]
-            for g in range(PASSES):
+            for c in range(PASSES):
                 w_words = stream.tile([P, OUT_COLS], U32, align_bytes=64)
+                block_rows = slice(BLOCK_ROWS * c, BLOCK_ROWS * (c + 1))
                 nc.sync.dma_start(
-                    out=w_words[:].bitcast(I32), in_=words[g].rearrange("p n t -> p (n t)").bitcast(I32)
+                    out=w_words[:].bitcast(I32),
+                    in_=words[:, block_rows].rearrange("g i n t -> g i (n t)").bitcast(I32),
                 )
                 for bank in range(BANKS):
                     cols = slice(bank * BANK_COLS, (bank + 1) * BANK_COLS)
                     nc.tensor.matmul_mx(
                         out=accs[bank][:],
-                        lhsT=h_words[:, g, :].bitcast(FP8X4),
-                        lhsT_scale=h_planes[:, g, :],
+                        lhsT=h_words[:, c, :].bitcast(FP8X4),
+                        lhsT_scale=h_planes[:, c, :],
                         rhs=w_words[:, cols].bitcast(FP8X4),
-                        rhs_scale=planes[name][QUADRANT_ROWS * (g % GROUP) : P, g // GROUP, cols],
-                        start=(g == 0),
-                        stop=(g == PASSES - 1),
+                        rhs_scale=planes[name][QUADRANT_ROWS * (c // PLANES) : P, c % PLANES, cols],
+                        start=(c == 0),
+                        stop=(c == PASSES - 1),
                     )
             results[name] = const.tile([P, HEADS, HEAD_DIM], F32, name="result_%s" % name)
             for bank in range(BANKS):

@@ -83,13 +83,14 @@ def rope_table(nc, const):
 
 
 def load_scale_planes(nc, planes, scales):
-    for quadrant in range(QUADRANTS):
-        first = QUADRANT * quadrant
-        groups = slice(QUADRANT_ROWS * quadrant, QUADRANT_ROWS * (quadrant + 1))
-        nc.gpsimd.dma_start(
-            out=planes[first : first + OFFSETS * QUADRANT_ROWS].rearrange("m f n -> m (f n)").bitcast(F32),
-            in_=scales[groups].rearrange("r (j f) n -> j r (f n)", f=PLANES).bitcast(F32),
-        )
+    for f in range(PLANES):
+        for quadrant in range(QUADRANTS):
+            first = QUADRANT * quadrant
+            groups = slice(QUADRANT_ROWS * quadrant, QUADRANT_ROWS * (quadrant + 1))
+            nc.gpsimd.dma_start(
+                out=planes[first : first + OFFSETS * QUADRANT_ROWS, f, :].bitcast(F32),
+                in_=scales[groups].rearrange("r (j f) n -> f j r n", f=PLANES)[f].bitcast(F32),
+            )
 
 
 def rotate_bank(nc, tail, table, acc, y):

@@ -26,6 +26,7 @@ PACK = 4
 K_PASS = P * PACK
 PASSES = DIM // K_PASS
 BLOCK_ROWS = 8
+QUARTERS = 4
 OUT_COLS = HEADS * HEAD_DIM
 BANK_COLS = 512
 BANKS = OUT_COLS // BANK_COLS
@@ -83,14 +84,13 @@ def rope_table(nc, const):
 
 
 def load_scale_planes(nc, planes, scales):
-    for f in range(PLANES):
-        for quadrant in range(QUADRANTS):
-            first = QUADRANT * quadrant
-            groups = slice(QUADRANT_ROWS * quadrant, QUADRANT_ROWS * (quadrant + 1))
-            nc.gpsimd.dma_start(
-                out=planes[first : first + OFFSETS * QUADRANT_ROWS, f, :].bitcast(F32),
-                in_=scales[groups].rearrange("r (j f) n -> f j r n", f=PLANES)[f].bitcast(F32),
-            )
+    by_quadrant = scales.rearrange("(j q) (r f) n -> q j r (f n)", q=QUADRANTS, f=PLANES)
+    for quadrant in range(QUADRANTS):
+        first = QUADRANT * quadrant
+        nc.gpsimd.dma_start(
+            out=planes[first : first + OFFSETS * QUADRANT_ROWS].rearrange("m f n -> m (f n)").bitcast(F32),
+            in_=by_quadrant[quadrant].bitcast(F32),
+        )
 
 
 def rotate_bank(nc, tail, table, acc, y):
@@ -128,10 +128,12 @@ def tile_flexattentionblock_pa_k_kernel(
 
         gain_rows = const.tile([PASSES, K_PASS], BF16)
         block = BLOCK_ROWS * PACK
-        nc.sync.dma_start(
-            out=gain_rows[:].rearrange("c (g u) -> c g u", u=block),
-            in_=attn_norm_w.rearrange("(g c u) -> c g u", c=PASSES, u=block),
-        )
+        gain_passes = attn_norm_w.rearrange("(j s f u) -> j f s u", j=QUARTERS, f=PLANES, u=block)
+        for j in range(QUARTERS):
+            nc.sync.dma_start(
+                out=gain_rows[PLANES * j : PLANES * (j + 1)].rearrange("f (s u) -> f s u", u=block),
+                in_=gain_passes[j],
+            )
         x_sb = const.tile([P, DIM], BF16)
         x_tokens = x.rearrange("b s d -> s b d")
         for c in range(X_CHUNKS):
@@ -184,15 +186,17 @@ def tile_flexattentionblock_pa_k_kernel(
 
         h_words = const.tile([P, PASSES, P], U32, align_bytes=64)
         h_planes = const.tile([P, PASSES, P], U8, align_bytes=64)
-        x_passes = x_sb[:].rearrange("m (g c i t) -> m c g i t", c=PASSES, i=BLOCK_ROWS, t=PACK)
+        x_passes = x_sb[:].rearrange(
+            "m (j s f i t) -> m j f s i t", j=QUARTERS, f=PLANES, i=BLOCK_ROWS, t=PACK
+        )
         for first_pass in range(0, PASSES, QUANTISED_TOGETHER):
             h_bf16 = head.tile([P, QUANTISED_TOGETHER, P, PACK], BF16, align_bytes=64)
             for j in range(QUANTISED_TOGETHER):
                 c = first_pass + j
                 x_scaled = head.tile([P, PACK, P], F32)
                 nc.scalar.activation(
-                    out=x_scaled[:].rearrange("m t (g i) -> m g i t", i=BLOCK_ROWS),
-                    in_=x_passes[:, c],
+                    out=x_scaled[:].rearrange("m t (s i) -> m s i t", i=BLOCK_ROWS),
+                    in_=x_passes[:, c // PLANES, c % PLANES],
                     func=ACT.Copy,
                     scale=inv_rms[:, 0:1],
                 )
@@ -214,13 +218,14 @@ def tile_flexattentionblock_pa_k_kernel(
 
         results = {}
         for name, words in (("q", wq_words), ("k", wk_words), ("v", wv_words)):
+            word_passes = words.rearrange(
+                "(j g) (r f i) n t -> j f (g r) i (n t)", j=QUARTERS, f=PLANES, i=BLOCK_ROWS
+            )
             accs = [psum_acc.tile([P, BANK_COLS], F32, name="acc_%s_%d" % (name, bank)) for bank in range(BANKS)]
             for c in range(PASSES):
                 w_words = stream.tile([P, OUT_COLS], U32, align_bytes=64)
-                block_rows = slice(BLOCK_ROWS * c, BLOCK_ROWS * (c + 1))
                 nc.sync.dma_start(
-                    out=w_words[:].bitcast(I32),
-                    in_=words[:, block_rows].rearrange("g i n t -> g i (n t)").bitcast(I32),
+                    out=w_words[:].bitcast(I32), in_=word_passes[c // PLANES, c % PLANES].bitcast(I32)
                 )
                 for bank in range(BANKS):
                     cols = slice(bank * BANK_COLS, (bank + 1) * BANK_COLS)

@@ -25,20 +25,17 @@ P = 128
 PACK = 4
 K_PASS = P * PACK
 PASSES = DIM // K_PASS
-BLOCK_ROWS = 8
-QUARTERS = 4
 OUT_COLS = HEADS * HEAD_DIM
 BANK_COLS = 512
 BANKS = OUT_COLS // BANK_COLS
 BANK_HEADS = BANK_COLS // HEAD_DIM
 PAIRS = HEAD_DIM // 2
 DOUBLINGS = 6
+GROUP = 4
+GROUPS = PASSES // GROUP
 QUADRANT = 32
 QUADRANTS = P // QUADRANT
 QUADRANT_ROWS = 4
-OFFSETS = 4
-PLANES = PASSES // OFFSETS
-QUANTISED_TOGETHER = 4
 X_CHUNKS = 4
 X_CHUNK = DIM // X_CHUNKS
 STREAM_BUFS = 32
@@ -84,13 +81,14 @@ def rope_table(nc, const):
 
 
 def load_scale_planes(nc, planes, scales):
-    by_quadrant = scales.rearrange("(j q) (r f) n -> q j r (f n)", q=QUADRANTS, f=PLANES)
-    for quadrant in range(QUADRANTS):
-        first = QUADRANT * quadrant
-        nc.gpsimd.dma_start(
-            out=planes[first : first + OFFSETS * QUADRANT_ROWS].rearrange("m f n -> m (f n)").bitcast(F32),
-            in_=by_quadrant[quadrant].bitcast(F32),
-        )
+    for a in range(GROUPS):
+        for quadrant in range(QUADRANTS):
+            first = QUADRANT * quadrant
+            rows = slice(QUADRANT_ROWS * quadrant, QUADRANT_ROWS * (quadrant + 1))
+            nc.gpsimd.dma_start(
+                out=planes[first : first + GROUP * QUADRANT_ROWS, a, :].bitcast(F32),
+                in_=scales[GROUP * a : GROUP * (a + 1), rows, :].bitcast(F32),
+            )
 
 
 def rotate_bank(nc, tail, table, acc, y):
@@ -127,13 +125,7 @@ def tile_flexattentionblock_pa_k_kernel(
         psum_acc = ctx.enter_context(tc.psum_pool(name="psum_acc", bufs=1))
 
         gain_rows = const.tile([PASSES, K_PASS], BF16)
-        block = BLOCK_ROWS * PACK
-        gain_passes = attn_norm_w.rearrange("(j s f u) -> j f s u", j=QUARTERS, f=PLANES, u=block)
-        for j in range(QUARTERS):
-            nc.sync.dma_start(
-                out=gain_rows[PLANES * j : PLANES * (j + 1)].rearrange("f (s u) -> f s u", u=block),
-                in_=gain_passes[j],
-            )
+        nc.sync.dma_start(out=gain_rows[:], in_=attn_norm_w.rearrange("(g c) -> g c", c=K_PASS))
         x_sb = const.tile([P, DIM], BF16)
         x_tokens = x.rearrange("b s d -> s b d")
         for c in range(X_CHUNKS):
@@ -143,7 +135,7 @@ def tile_flexattentionblock_pa_k_kernel(
         scale_inputs = {"q": wq_scales, "k": wk_scales, "v": wv_scales}
         planes = {}
         for name in ("q", "k", "v"):
-            planes[name] = const.tile([P, PLANES, OUT_COLS], U8, align_bytes=64, name="planes_%s" % name)
+            planes[name] = const.tile([P, GROUPS, OUT_COLS], U8, align_bytes=64, name="planes_%s" % name)
             nc.vector.memset(planes[name][:].bitcast(I32), 0)
 
         table = rope_table(nc, const)
@@ -155,14 +147,14 @@ def tile_flexattentionblock_pa_k_kernel(
         gain_sorted = const.tile([P, PACK, P], F32)
         nc.vector.memset(gain_sorted[:], 0.0)
         nc.vector.tensor_copy(
-            out=gain_sorted[0:PASSES].rearrange("c t p -> c p t"),
-            in_=gain_rows[:].rearrange("c (p t) -> c p t", t=PACK),
+            out=gain_sorted[0:PASSES].rearrange("g t p -> g p t"),
+            in_=gain_rows[:].rearrange("g (p t) -> g p t", t=PACK),
         )
         gain_t = psum_t.tile([P, PACK, P], F32, tag="transposed")
         for t in range(PACK):
             nc.tensor.transpose(out=gain_t[:, t, :], in_=gain_sorted[:, t, :], identity=identity[:])
         gain = const.tile([P, PASSES, PACK], F32)
-        nc.vector.tensor_copy(out=gain[:], in_=gain_t[:, :, 0:PASSES].rearrange("p t c -> p c t"))
+        nc.vector.tensor_copy(out=gain[:], in_=gain_t[:, :, 0:PASSES].rearrange("p t g -> p g t"))
 
         square_sums = const.tile([P, X_CHUNKS], F32)
         for c in range(X_CHUNKS):
@@ -186,17 +178,14 @@ def tile_flexattentionblock_pa_k_kernel(
 
         h_words = const.tile([P, PASSES, P], U32, align_bytes=64)
         h_planes = const.tile([P, PASSES, P], U8, align_bytes=64)
-        x_passes = x_sb[:].rearrange(
-            "m (j s f i t) -> m j f s i t", j=QUARTERS, f=PLANES, i=BLOCK_ROWS, t=PACK
-        )
-        for first_pass in range(0, PASSES, QUANTISED_TOGETHER):
-            h_bf16 = head.tile([P, QUANTISED_TOGETHER, P, PACK], BF16, align_bytes=64)
-            for j in range(QUANTISED_TOGETHER):
-                c = first_pass + j
+        for a in range(GROUPS):
+            h_bf16 = head.tile([P, GROUP, P, PACK], BF16, align_bytes=64)
+            for j in range(GROUP):
+                g = GROUP * a + j
                 x_scaled = head.tile([P, PACK, P], F32)
                 nc.scalar.activation(
-                    out=x_scaled[:].rearrange("m t (s i) -> m s i t", i=BLOCK_ROWS),
-                    in_=x_passes[:, c // PLANES, c % PLANES],
+                    out=x_scaled[:].rearrange("m t p -> m p t"),
+                    in_=x_sb[:, g * K_PASS : (g + 1) * K_PASS].rearrange("m (p t) -> m p t", t=PACK),
                     func=ACT.Copy,
                     scale=inv_rms[:, 0:1],
                 )
@@ -206,37 +195,34 @@ def tile_flexattentionblock_pa_k_kernel(
                 nc.vector.tensor_tensor(
                     out=h_bf16[:, j],
                     in0=x_t[:].rearrange("p t m -> p m t"),
-                    in1=gain[:, c, :].unsqueeze(1).to_broadcast([P, P, PACK]),
+                    in1=gain[:, g, :].unsqueeze(1).to_broadcast([P, P, PACK]),
                     op=ALU.mult,
                 )
-            together = slice(first_pass, first_pass + QUANTISED_TOGETHER)
+            group = slice(GROUP * a, GROUP * (a + 1))
             nc.vector.quantize_mx(
-                out=h_words[:, together, :].rearrange("p c m -> p (c m)").bitcast(FP8X4),
-                scales=h_planes[:, together, :].rearrange("p c m -> p (c m)"),
+                out=h_words[:, group, :].rearrange("p g m -> p (g m)").bitcast(FP8X4),
+                scales=h_planes[:, group, :].rearrange("p g m -> p (g m)"),
                 in_=h_bf16[:].rearrange("p j m t -> p (j m t)"),
             )
 
         results = {}
         for name, words in (("q", wq_words), ("k", wk_words), ("v", wv_words)):
-            word_passes = words.rearrange(
-                "(j g) (r f i) n t -> j f (g r) i (n t)", j=QUARTERS, f=PLANES, i=BLOCK_ROWS
-            )
             accs = [psum_acc.tile([P, BANK_COLS], F32, name="acc_%s_%d" % (name, bank)) for bank in range(BANKS)]
-            for c in range(PASSES):
+            for g in range(PASSES):
                 w_words = stream.tile([P, OUT_COLS], U32, align_bytes=64)
                 nc.sync.dma_start(
-                    out=w_words[:].bitcast(I32), in_=word_passes[c // PLANES, c % PLANES].bitcast(I32)
+                    out=w_words[:].bitcast(I32), in_=words[g].rearrange("p n t -> p (n t)").bitcast(I32)
                 )
                 for bank in range(BANKS):
                     cols = slice(bank * BANK_COLS, (bank + 1) * BANK_COLS)
                     nc.tensor.matmul_mx(
                         out=accs[bank][:],
-                        lhsT=h_words[:, c, :].bitcast(FP8X4),
-                        lhsT_scale=h_planes[:, c, :],
+                        lhsT=h_words[:, g, :].bitcast(FP8X4),
+                        lhsT_scale=h_planes[:, g, :],
                         rhs=w_words[:, cols].bitcast(FP8X4),
-                        rhs_scale=planes[name][QUADRANT_ROWS * (c // PLANES) : P, c % PLANES, cols],
-                        start=(c == 0),
-                        stop=(c == PASSES - 1),
+                        rhs_scale=planes[name][QUADRANT_ROWS * (g % GROUP) : P, g // GROUP, cols],
+                        start=(g == 0),
+                        stop=(g == PASSES - 1),
                     )
             results[name] = const.tile([P, HEADS, HEAD_DIM], F32, name="result_%s" % name)
             for bank in range(BANKS):
@@ -249,5 +235,9 @@ def tile_flexattentionblock_pa_k_kernel(
                     nc.scalar.copy(out=y.rearrange("m h f -> m (h f)"), in_=accs[bank][:])
 
         for name, out in (("q", out_0), ("k", out_1), ("v", out_2)):
-            for b in range(BATCH):
-                nc.sync.dma_start(out=out[b].rearrange("h s f -> s h f"), in_=results[name][b:P:BATCH])
+            for bank in range(BANKS):
+                heads = slice(bank * BANK_HEADS, (bank + 1) * BANK_HEADS)
+                for b in range(BATCH):
+                    nc.sync.dma_start(
+                        out=out[b, heads].rearrange("h s f -> s h f"), in_=results[name][b:P:BATCH, heads, :]
+                    )

@@ -38,7 +38,7 @@ QUADRANTS = P // QUADRANT
 QUADRANT_ROWS = 4
 X_CHUNKS = 4
 X_CHUNK = DIM // X_CHUNKS
-STREAM_BUFS = 32
+STREAM_BUFS = 8
 
 ROUND_MAGIC = 1.5 * 2.0**23
 
@@ -209,10 +209,16 @@ def tile_flexattentionblock_pa_k_kernel(
         for name, words in (("q", wq_words), ("k", wk_words), ("v", wv_words)):
             accs = [psum_acc.tile([P, BANK_COLS], F32, name="acc_%s_%d" % (name, bank)) for bank in range(BANKS)]
             for g in range(PASSES):
-                w_words = stream.tile([P, OUT_COLS], U32, align_bytes=64)
-                nc.sync.dma_start(
-                    out=w_words[:].bitcast(I32), in_=words[g].rearrange("p n t -> p (n t)").bitcast(I32)
-                )
+                j = g % GROUP
+                if j == 0:
+                    w_group = stream.tile([P, GROUP, OUT_COLS], U32, align_bytes=64)
+                    last_group = name == "v" and g == PASSES - GROUP
+                    for first, count in ((0, 2), (2, 1), (3, 1)) if last_group else ((0, GROUP),):
+                        nc.sync.dma_start(
+                            out=w_group[:, first : first + count, :].bitcast(I32),
+                            in_=words[g + first : g + first + count].rearrange("g p n t -> p g (n t)").bitcast(I32),
+                        )
+                w_words = w_group[:, j, :]
                 for bank in range(BANKS):
                     cols = slice(bank * BANK_COLS, (bank + 1) * BANK_COLS)
                     nc.tensor.matmul_mx(

@@ -40,6 +40,11 @@ X_CHUNKS = 4
 X_CHUNK = DIM // X_CHUNKS
 STREAM_BUFS = 8
 
+PIECES = {
+    ("v", GROUPS - 2): ((0, 2, 0, BANKS), (2, 2, 0, BANKS)),
+    ("v", GROUPS - 1): ((0, 1, 0, BANKS), (1, 1, 0, BANKS), (2, 1, 0, BANKS), (3, 1, 0, 1), (3, 1, 1, 1)),
+}
+
 ROUND_MAGIC = 1.5 * 2.0**23
 
 FLOPS = 2 * P * DIM * 3 * OUT_COLS
@@ -212,11 +217,11 @@ def tile_flexattentionblock_pa_k_kernel(
                 j = g % GROUP
                 if j == 0:
                     w_group = stream.tile([P, GROUP, OUT_COLS], U32, align_bytes=64)
-                    last_group = name == "v" and g == PASSES - GROUP
-                    for first, count in ((0, 2), (2, 1), (3, 1)) if last_group else ((0, GROUP),):
+                    for first, count, first_bank, banks in PIECES.get((name, g // GROUP), ((0, GROUP, 0, BANKS),)):
+                        cols = slice(first_bank * BANK_COLS, (first_bank + banks) * BANK_COLS)
+                        source = words[g + first : g + first + count].rearrange("g p n t -> p g (n t)").bitcast(I32)
                         nc.sync.dma_start(
-                            out=w_group[:, first : first + count, :].bitcast(I32),
-                            in_=words[g + first : g + first + count].rearrange("g p n t -> p g (n t)").bitcast(I32),
+                            out=w_group[:, first : first + count, cols].bitcast(I32), in_=source[:, :, cols]
                         )
                 w_words = w_group[:, j, :]
                 for bank in range(BANKS):
@@ -240,10 +245,10 @@ def tile_flexattentionblock_pa_k_kernel(
                 else:
                     nc.scalar.copy(out=y.rearrange("m h f -> m (h f)"), in_=accs[bank][:])
 
-        for name, out in (("q", out_0), ("k", out_1), ("v", out_2)):
-            for bank in range(BANKS):
-                heads = slice(bank * BANK_HEADS, (bank + 1) * BANK_HEADS)
-                for b in range(BATCH):
-                    nc.sync.dma_start(
-                        out=out[b, heads].rearrange("h s f -> s h f"), in_=results[name][b:P:BATCH, heads, :]
-                    )
+        for name, out in (("q", out_0), ("k", out_1)):
+            for b in range(BATCH):
+                nc.sync.dma_start(out=out[b].rearrange("h s f -> s h f"), in_=results[name][b:P:BATCH, :, :])
+        for bank, queue in ((0, nc.sync), (1, nc.scalar)):
+            heads = slice(bank * BANK_HEADS, (bank + 1) * BANK_HEADS)
+            for b in range(BATCH):
+                queue.dma_start(out=out_2[b, heads].rearrange("h s f -> s h f"), in_=results["v"][b:P:BATCH, heads, :])

@@ -53,9 +53,7 @@ assert P == BATCH * SEQ
 assert 2**DOUBLINGS == PAIRS
 
 
-def rope_table(nc, const):
-    partition = const.tile([P, 1], I32)
-    nc.gpsimd.iota(partition[:], pattern=[[0, 1]], base=0, channel_multiplier=1)
+def rope_table(nc, const, partition):
     position = const.tile([P, 1], I32)
     nc.vector.tensor_single_scalar(out=position[:], in_=partition[:], scalar=1, op=ALU.arith_shift_right)
 
@@ -137,13 +135,19 @@ def tile_flexattentionblock_pa_k_kernel(
             cols = slice(c * X_CHUNK, (c + 1) * X_CHUNK)
             nc.sync.dma_start(out=x_sb[:, cols], in_=x_tokens[:, :, cols])
 
+        one = const.tile([P, 1], F32)
+        nc.vector.memset(one[:], 1.0)
+        warm = const.tile([P, 1], F32)
+        nc.scalar.activation(out=warm[:], in_=one[:], func=ACT.Sqrt)
+
         scale_inputs = {"q": wq_scales, "k": wk_scales, "v": wv_scales}
         planes = {}
         for name in ("q", "k", "v"):
             planes[name] = const.tile([P, GROUPS, OUT_COLS], U8, align_bytes=64, name="planes_%s" % name)
             nc.vector.memset(planes[name][:].bitcast(I32), 0)
 
-        table = rope_table(nc, const)
+        partition = const.tile([P, 1], I32)
+        nc.gpsimd.iota(partition[:], pattern=[[0, 1]], base=0, channel_multiplier=1)
         identity = const.tile([P, P], F32)
         make_identity(nc, identity[:])
         for name in ("q", "k", "v"):
@@ -161,17 +165,33 @@ def tile_flexattentionblock_pa_k_kernel(
         gain = const.tile([P, PASSES, PACK], F32)
         nc.vector.tensor_copy(out=gain[:], in_=gain_t[:, :, 0:PASSES].rearrange("p t g -> p g t"))
 
-        square_sums = const.tile([P, X_CHUNKS], F32)
+        square_sums = const.tile([P, X_CHUNKS // 2, 3], F32)
         for c in range(X_CHUNKS):
-            squares = head.tile([P, X_CHUNK], BF16)
-            nc.scalar.activation(
-                out=squares[:],
-                in_=x_sb[:, c * X_CHUNK : (c + 1) * X_CHUNK],
-                func=ACT.Square,
-                accum_out=square_sums[:, c : c + 1],
-            )
+            if c % 2 == 0:
+                squares = head.tile([P, X_CHUNK], BF16)
+                nc.scalar.activation(
+                    out=squares[:],
+                    in_=x_sb[:, c * X_CHUNK : (c + 1) * X_CHUNK],
+                    func=ACT.Square,
+                    accum_out=square_sums[:, c // 2, 0:1],
+                )
+            else:
+                for half in range(2):
+                    cols = slice(c * X_CHUNK + half * (X_CHUNK // 2), c * X_CHUNK + (half + 1) * (X_CHUNK // 2))
+                    squares = head.tile([P, X_CHUNK // 2], F32)
+                    nc.vector.scalar_tensor_tensor(
+                        out=squares[:],
+                        in0=x_sb[:, cols],
+                        scalar=1.0,
+                        in1=x_sb[:, cols],
+                        op0=ALU.mult,
+                        op1=ALU.mult,
+                        accum_out=square_sums[:, c // 2, 1 + half : 2 + half],
+                    )
         square_sum = const.tile([P, 1], F32)
-        nc.vector.tensor_reduce(out=square_sum[:], in_=square_sums[:], axis=mybir.AxisListType.X, op=ALU.add)
+        nc.vector.tensor_reduce(
+            out=square_sum[:], in_=square_sums[:].rearrange("m c e -> m (c e)"), axis=mybir.AxisListType.X, op=ALU.add
+        )
         mean_square = const.tile([P, 1], F32)
         nc.vector.tensor_scalar(
             out=mean_square[:], in0=square_sum[:], scalar1=1.0 / DIM, scalar2=EPS, op0=ALU.mult, op1=ALU.add
@@ -209,6 +229,8 @@ def tile_flexattentionblock_pa_k_kernel(
                 scales=h_planes[:, group, :].rearrange("p g m -> p (g m)"),
                 in_=h_bf16[:].rearrange("p j m t -> p (j m t)"),
             )
+
+        table = rope_table(nc, const, partition)
 
         results = {}
         for name, words in (("q", wq_words), ("k", wk_words), ("v", wv_words)):

@@ -131,9 +131,7 @@ def tile_flexattentionblock_pa_k_kernel(
         nc.sync.dma_start(out=gain_rows[:], in_=attn_norm_w.rearrange("(g c) -> g c", c=K_PASS))
         x_sb = const.tile([P, DIM], BF16)
         x_tokens = x.rearrange("b s d -> s b d")
-        for c in range(X_CHUNKS):
-            cols = slice(c * X_CHUNK, (c + 1) * X_CHUNK)
-            nc.sync.dma_start(out=x_sb[:, cols], in_=x_tokens[:, :, cols])
+        nc.sync.dma_start(out=x_sb[:], in_=x_tokens)
 
         one = const.tile([P, 1], F32)
         nc.vector.memset(one[:], 1.0)

@@ -45,6 +45,8 @@ PIECES = {
     ("v", GROUPS - 1): ((0, 1, 0, BANKS), (1, 1, 0, BANKS), (2, 1, 0, BANKS), (3, 1, 0, 1), (3, 1, 1, 1)),
 }
 
+DMA_ALIGN = 256
+
 ROUND_MAGIC = 1.5 * 2.0**23
 
 FLOPS = 2 * P * DIM * 3 * OUT_COLS
@@ -129,7 +131,7 @@ def tile_flexattentionblock_pa_k_kernel(
 
         gain_rows = const.tile([PASSES, K_PASS], BF16)
         nc.sync.dma_start(out=gain_rows[:], in_=attn_norm_w.rearrange("(g c) -> g c", c=K_PASS))
-        x_sb = const.tile([P, DIM], BF16)
+        x_sb = const.tile([P, DIM], BF16, align_bytes=DMA_ALIGN)
         x_tokens = x.rearrange("b s d -> s b d")
         nc.sync.dma_start(out=x_sb[:], in_=x_tokens)
 
@@ -141,7 +143,7 @@ def tile_flexattentionblock_pa_k_kernel(
         scale_inputs = {"q": wq_scales, "k": wk_scales, "v": wv_scales}
         planes = {}
         for name in ("q", "k", "v"):
-            planes[name] = const.tile([P, GROUPS, OUT_COLS], U8, align_bytes=64, name="planes_%s" % name)
+            planes[name] = const.tile([P, GROUPS, OUT_COLS], U8, align_bytes=DMA_ALIGN, name="planes_%s" % name)
             nc.vector.memset(planes[name][:].bitcast(I32), 0)
 
         partition = const.tile([P, 1], I32)
@@ -236,7 +238,7 @@ def tile_flexattentionblock_pa_k_kernel(
             for g in range(PASSES):
                 j = g % GROUP
                 if j == 0:
-                    w_group = stream.tile([P, GROUP, OUT_COLS], U32, align_bytes=64)
+                    w_group = stream.tile([P, GROUP, OUT_COLS], U32, align_bytes=DMA_ALIGN)
                     for first, count, first_bank, banks in PIECES.get((name, g // GROUP), ((0, GROUP, 0, BANKS),)):
                         cols = slice(first_bank * BANK_COLS, (first_bank + banks) * BANK_COLS)
                         source = words[g + first : g + first + count].rearrange("g p n t -> p g (n t)").bitcast(I32)
@@ -255,7 +257,7 @@ def tile_flexattentionblock_pa_k_kernel(
                         start=(g == 0),
                         stop=(g == PASSES - 1),
                     )
-            results[name] = const.tile([P, HEADS, HEAD_DIM], F32, name="result_%s" % name)
+            results[name] = const.tile([P, HEADS, HEAD_DIM], F32, align_bytes=DMA_ALIGN, name="result_%s" % name)
             for bank in range(BANKS):
                 y = results[name][:, bank * BANK_HEADS : (bank + 1) * BANK_HEADS, :]
                 if name != "v":

@@ -46,6 +46,7 @@ PIECES = {
 }
 
 DMA_ALIGN = 256
+PIECE_ALIGN = 4096
 
 ROUND_MAGIC = 1.5 * 2.0**23
 
@@ -131,7 +132,7 @@ def tile_flexattentionblock_pa_k_kernel(
 
         gain_rows = const.tile([PASSES, K_PASS], BF16)
         nc.sync.dma_start(out=gain_rows[:], in_=attn_norm_w.rearrange("(g c) -> g c", c=K_PASS))
-        x_sb = const.tile([P, DIM], BF16, align_bytes=DMA_ALIGN)
+        x_sb = const.tile([P, DIM], BF16, align_bytes=PIECE_ALIGN)
         x_tokens = x.rearrange("b s d -> s b d")
         nc.sync.dma_start(out=x_sb[:], in_=x_tokens)
 
@@ -238,7 +239,7 @@ def tile_flexattentionblock_pa_k_kernel(
             for g in range(PASSES):
                 j = g % GROUP
                 if j == 0:
-                    w_group = stream.tile([P, GROUP, OUT_COLS], U32, align_bytes=DMA_ALIGN)
+                    w_group = stream.tile([P, GROUP, OUT_COLS], U32, align_bytes=PIECE_ALIGN)
                     for first, count, first_bank, banks in PIECES.get((name, g // GROUP), ((0, GROUP, 0, BANKS),)):
                         cols = slice(first_bank * BANK_COLS, (first_bank + banks) * BANK_COLS)
                         source = words[g + first : g + first + count].rearrange("g p n t -> p g (n t)").bitcast(I32)

import math
from contextlib import ExitStack

import concourse.mybir as mybir
from concourse.masks import make_identity

F32 = mybir.dt.float32
BF16 = mybir.dt.bfloat16
I32 = mybir.dt.int32
U32 = mybir.dt.uint32
U8 = mybir.dt.uint8
FP8X4 = mybir.dt.float8_e4m3fn_x4
ALU = mybir.AluOpType
ACT = mybir.ActivationFunctionType

BATCH = 2
SEQ = 64
DIM = 8192
HEADS = 8
HEAD_DIM = 128
THETA = 10000.0
EPS = 1e-6

P = 128
PACK = 4
K_PASS = P * PACK
PASSES = DIM // K_PASS
OUT_COLS = HEADS * HEAD_DIM
BANK_COLS = 512
BANKS = OUT_COLS // BANK_COLS
BANK_HEADS = BANK_COLS // HEAD_DIM
PAIRS = HEAD_DIM // 2
DOUBLINGS = 6
GROUP = 4
GROUPS = PASSES // GROUP
QUADRANT = 32
QUADRANTS = P // QUADRANT
QUADRANT_ROWS = 4
X_CHUNKS = 4
X_CHUNK = DIM // X_CHUNKS
STREAM_BUFS = 8

PIECES = {
    ("v", GROUPS - 2): ((0, 2, 0, BANKS), (2, 2, 0, BANKS)),
    ("v", GROUPS - 1): ((0, 1, 0, BANKS), (1, 1, 0, BANKS), (2, 1, 0, BANKS), (3, 1, 0, 1), (3, 1, 1, 1)),
}

DMA_ALIGN = 256
PIECE_ALIGN = 4096

ROUND_MAGIC = 1.5 * 2.0**23

FLOPS = 2 * P * DIM * 3 * OUT_COLS

assert P == BATCH * SEQ
assert 2**DOUBLINGS == PAIRS


def rope_table(nc, const, partition):
    position = const.tile([P, 1], I32)
    nc.vector.tensor_single_scalar(out=position[:], in_=partition[:], scalar=1, op=ALU.arith_shift_right)

    turns = const.tile([P, PAIRS], F32)
    nc.vector.tensor_scalar(
        out=turns[:, 0:1], in0=position[:], scalar1=1.0 / (2.0 * math.pi), scalar2=None, op0=ALU.mult
    )
    ratio = THETA ** (-2.0 / HEAD_DIM)
    for step in range(DOUBLINGS):
        width = 2**step
        nc.vector.tensor_scalar(
            out=turns[:, width : 2 * width], in0=turns[:, 0:width], scalar1=ratio**width, scalar2=None, op0=ALU.mult
        )

    twice = turns[:].unsqueeze(2).to_broadcast([P, PAIRS, 2])
    phase = const.tile([P, 2, PAIRS, 2], F32)
    nc.vector.tensor_scalar(out=phase[:, 0], in0=twice, scalar1=0.25, scalar2=None, op0=ALU.add)
    nc.vector.tensor_copy(out=phase[:, 1], in_=twice)
    whole = const.tile([P, 2, PAIRS, 2], F32)
    nc.vector.tensor_scalar(
        out=whole[:], in0=phase[:], scalar1=ROUND_MAGIC, scalar2=ROUND_MAGIC, op0=ALU.add, op1=ALU.subtract
    )
    fraction = const.tile([P, 2, PAIRS, 2], F32)
    nc.vector.tensor_tensor(out=fraction[:], in0=phase[:], in1=whole[:], op=ALU.subtract)
    table = const.tile([P, 2, PAIRS, 2], F32)
    nc.scalar.activation(out=table[:], in_=fraction[:], func=ACT.Sin, scale=2.0 * math.pi)
    return table


def load_scale_planes(nc, planes, scales):
    for a in range(GROUPS):
        for quadrant in range(QUADRANTS):
            first = QUADRANT * quadrant
            rows = slice(QUADRANT_ROWS * quadrant, QUADRANT_ROWS * (quadrant + 1))
            nc.gpsimd.dma_start(
                out=planes[first : first + GROUP * QUADRANT_ROWS, a, :].bitcast(F32),
                in_=scales[GROUP * a : GROUP * (a + 1), rows, :].bitcast(F32),
            )


def rotate_bank(nc, tail, table, acc, y):
    def over_heads(cos_or_sin):
        return cos_or_sin.rearrange("m j e -> m (j e)").unsqueeze(1).to_broadcast([P, BANK_HEADS, HEAD_DIM])

    def pairs(tile_ap):
        return tile_ap.rearrange("m h (j e) -> m (h j) e", e=2)

    u = acc[:].rearrange("m (h f) -> m h f", f=HEAD_DIM)
    u_cos = tail.tile([P, BANK_HEADS, HEAD_DIM], F32)
    nc.vector.tensor_tensor(out=u_cos[:], in0=u, in1=over_heads(table[:, 0]), op=ALU.mult)
    u_sin = tail.tile([P, BANK_HEADS, HEAD_DIM], F32)
    nc.vector.tensor_tensor(out=u_sin[:], in0=u, in1=over_heads(table[:, 1]), op=ALU.mult)
    nc.vector.tensor_tensor(
        out=pairs(y)[:, :, 0], in0=pairs(u_cos[:])[:, :, 0], in1=pairs(u_sin[:])[:, :, 1], op=ALU.subtract
    )
    nc.vector.tensor_tensor(
        out=pairs(y)[:, :, 1], in0=pairs(u_cos[:])[:, :, 1], in1=pairs(u_sin[:])[:, :, 0], op=ALU.add
    )


def tile_flexattentionblock_pa_k_kernel(
    tc, x, attn_norm_w, wq_words, wq_scales, wk_words, wk_scales, wv_words, wv_scales, out_0, out_1, out_2
):
    nc = tc.nc
    with ExitStack() as ctx:
        ctx.enter_context(tc.manual_schedule())
        const = ctx.enter_context(tc.tile_pool(name="const", bufs=1))
        head = ctx.enter_context(tc.tile_pool(name="head", bufs=3))
        stream = ctx.enter_context(tc.tile_pool(name="stream", bufs=STREAM_BUFS))
        tail = ctx.enter_context(tc.tile_pool(name="tail", bufs=2))
        psum_t = ctx.enter_context(tc.psum_pool(name="psum_t", bufs=2))
        psum_acc = ctx.enter_context(tc.psum_pool(name="psum_acc", bufs=1))

        gain_rows = const.tile([PASSES, K_PASS], BF16)
        nc.sync.dma_start(out=gain_rows[:], in_=attn_norm_w.rearrange("(g c) -> g c", c=K_PASS))
        x_sb = const.tile([P, DIM], BF16, align_bytes=PIECE_ALIGN)
        x_tokens = x.rearrange("b s d -> s b d")
        nc.sync.dma_start(out=x_sb[:], in_=x_tokens)

        one = const.tile([P, 1], F32)
        nc.vector.memset(one[:], 1.0)
        warm = const.tile([P, 1], F32)
        nc.scalar.activation(out=warm[:], in_=one[:], func=ACT.Sqrt)

        scale_inputs = {"q": wq_scales, "k": wk_scales, "v": wv_scales}
        planes = {}
        for name in ("q", "k", "v"):
            planes[name] = const.tile([P, GROUPS, OUT_COLS], U8, align_bytes=DMA_ALIGN, name="planes_%s" % name)
            nc.vector.memset(planes[name][:].bitcast(I32), 0)

        partition = const.tile([P, 1], I32)
        nc.gpsimd.iota(partition[:], pattern=[[0, 1]], base=0, channel_multiplier=1)
        identity = const.tile([P, P], F32)
        make_identity(nc, identity[:])
        for name in ("q", "k", "v"):
            load_scale_planes(nc, planes[name], scale_inputs[name])

        gain_sorted = const.tile([P, PACK, P], F32)
        nc.vector.memset(gain_sorted[:], 0.0)
        nc.vector.tensor_copy(
            out=gain_sorted[0:PASSES].rearrange("g t p -> g p t"),
            in_=gain_rows[:].rearrange("g (p t) -> g p t", t=PACK),
        )
        gain_t = psum_t.tile([P, PACK, P], F32, tag="transposed")
        for t in range(PACK):
            nc.tensor.transpose(out=gain_t[:, t, :], in_=gain_sorted[:, t, :], identity=identity[:])
        gain = const.tile([P, PASSES, PACK], F32)
        nc.vector.tensor_copy(out=gain[:], in_=gain_t[:, :, 0:PASSES].rearrange("p t g -> p g t"))

        square_sums = const.tile([P, X_CHUNKS // 2, 3], F32)
        for c in range(X_CHUNKS):
            if c % 2 == 0:
                squares = head.tile([P, X_CHUNK], BF16)
                nc.scalar.activation(
                    out=squares[:],
                    in_=x_sb[:, c * X_CHUNK : (c + 1) * X_CHUNK],
                    func=ACT.Square,
                    accum_out=square_sums[:, c // 2, 0:1],
                )
            else:
                for half in range(2):
                    cols = slice(c * X_CHUNK + half * (X_CHUNK // 2), c * X_CHUNK + (half + 1) * (X_CHUNK // 2))
                    squares = head.tile([P, X_CHUNK // 2], F32)
                    nc.vector.scalar_tensor_tensor(
                        out=squares[:],
                        in0=x_sb[:, cols],
                        scalar=1.0,
                        in1=x_sb[:, cols],
                        op0=ALU.mult,
                        op1=ALU.mult,
                        accum_out=square_sums[:, c // 2, 1 + half : 2 + half],
                    )
        square_sum = const.tile([P, 1], F32)
        nc.vector.tensor_reduce(
            out=square_sum[:], in_=square_sums[:].rearrange("m c e -> m (c e)"), axis=mybir.AxisListType.X, op=ALU.add
        )
        mean_square = const.tile([P, 1], F32)
        nc.vector.tensor_scalar(
            out=mean_square[:], in0=square_sum[:], scalar1=1.0 / DIM, scalar2=EPS, op0=ALU.mult, op1=ALU.add
        )
        rms = const.tile([P, 1], F32)
        nc.scalar.activation(out=rms[:], in_=mean_square[:], func=ACT.Sqrt)
        inv_rms = const.tile([P, 1], F32)
        nc.vector.reciprocal(out=inv_rms[:], in_=rms[:])

        h_words = const.tile([P, PASSES, P], U32, align_bytes=64)
        h_planes = const.tile([P, PASSES, P], U8, align_bytes=64)
        for a in range(GROUPS):
            h_bf16 = head.tile([P, GROUP, P, PACK], BF16, align_bytes=64)
            for j in range(GROUP):
                g = GROUP * a + j
                x_scaled = head.tile([P, PACK, P], F32)
                nc.scalar.activation(
                    out=x_scaled[:].rearrange("m t p -> m p t"),
                    in_=x_sb[:, g * K_PASS : (g + 1) * K_PASS].rearrange("m (p t) -> m p t", t=PACK),
                    func=ACT.Copy,
                    scale=inv_rms[:, 0:1],
                )
                x_t = psum_t.tile([P, PACK, P], F32, tag="transposed")
                for t in range(PACK):
                    nc.tensor.transpose(out=x_t[:, t, :], in_=x_scaled[:, t, :], identity=identity[:])
                nc.vector.tensor_tensor(
                    out=h_bf16[:, j],
                    in0=x_t[:].rearrange("p t m -> p m t"),
                    in1=gain[:, g, :].unsqueeze(1).to_broadcast([P, P, PACK]),
                    op=ALU.mult,
                )
            group = slice(GROUP * a, GROUP * (a + 1))
            nc.vector.quantize_mx(
                out=h_words[:, group, :].rearrange("p g m -> p (g m)").bitcast(FP8X4),
                scales=h_planes[:, group, :].rearrange("p g m -> p (g m)"),
                in_=h_bf16[:].rearrange("p j m t -> p (j m t)"),
            )

        table = rope_table(nc, const, partition)

        results = {}
        for name, words in (("q", wq_words), ("k", wk_words), ("v", wv_words)):
            accs = [psum_acc.tile([P, BANK_COLS], F32, name="acc_%s_%d" % (name, bank)) for bank in range(BANKS)]
            for g in range(PASSES):
                j = g % GROUP
                if j == 0:
                    w_group = stream.tile([P, GROUP, OUT_COLS], U32, align_bytes=PIECE_ALIGN)
                    for first, count, first_bank, banks in PIECES.get((name, g // GROUP), ((0, GROUP, 0, BANKS),)):
                        cols = slice(first_bank * BANK_COLS, (first_bank + banks) * BANK_COLS)
                        source = words[g + first : g + first + count].rearrange("g p n t -> p g (n t)").bitcast(I32)
                        nc.sync.dma_start(
                            out=w_group[:, first : first + count, cols].bitcast(I32), in_=source[:, :, cols]
                        )
                w_words = w_group[:, j, :]
                for bank in range(BANKS):
                    cols = slice(bank * BANK_COLS, (bank + 1) * BANK_COLS)
                    nc.tensor.matmul_mx(
                        out=accs[bank][:],
                        lhsT=h_words[:, g, :].bitcast(FP8X4),
                        lhsT_scale=h_planes[:, g, :],
                        rhs=w_words[:, cols].bitcast(FP8X4),
                        rhs_scale=planes[name][QUADRANT_ROWS * (g % GROUP) : P, g // GROUP, cols],
                        start=(g == 0),
                        stop=(g == PASSES - 1),
                    )
            results[name] = const.tile([P, HEADS, HEAD_DIM], F32, align_bytes=DMA_ALIGN, name="result_%s" % name)
            for bank in range(BANKS):
                y = results[name][:, bank * BANK_HEADS : (bank + 1) * BANK_HEADS, :]
                if name != "v":
                    rotate_bank(nc, tail, table, accs[bank], y)
                elif bank == 0:
                    nc.vector.tensor_copy(out=y.rearrange("m h f -> m (h f)"), in_=accs[bank][:])
                else:
                    nc.scalar.copy(out=y.rearrange("m h f -> m (h f)"), in_=accs[bank][:])

        for name, out in (("q", out_0), ("k", out_1)):
            for b in range(BATCH):
                nc.sync.dma_start(out=out[b].rearrange("h s f -> s h f"), in_=results[name][b:P:BATCH, :, :])
        for bank, queue in ((0, nc.sync), (1, nc.scalar)):
            heads = slice(bank * BANK_HEADS, (bank + 1) * BANK_HEADS)
            for b in range(BATCH):
                queue.dma_start(out=out_2[b, heads].rearrange("h s f -> s h f"), in_=results["v"][b:P:BATCH, heads, :])
